import numpy as np
import ml_dtypes


def mxq(x, axis, fmt="e4m3"):
    dtype, down = {"e4m3": (ml_dtypes.float8_e4m3fn, 7), "e5m2": (ml_dtypes.float8_e5m2, 14)}[fmt]
    v = np.moveaxis(np.asarray(x, np.float32).astype(ml_dtypes.bfloat16).astype(np.float64), axis, -1)
    blocks = v.reshape(v.shape[:-1] + (-1, 32))
    amax = np.abs(blocks).max(-1, keepdims=True)
    byte = np.maximum(np.where(amax > 0, np.frexp(amax)[1] - 1 + 127, 0) - down, 1)
    scale = np.exp2(byte - 127.0)
    codes = (blocks / scale).astype(np.float32).astype(dtype).astype(np.float64)
    return np.moveaxis((codes * scale).reshape(v.shape), -1, axis)


WIDE = False


def mx_kscale(k):
    if not WIDE:
        return np.ones(k)
    levels = np.array([10, -10, 5, -5, 0])
    a = np.random.permutation(np.resize(levels, k // 512 * 4)).reshape(k // 512, 4)
    idx = np.arange(k)
    return np.exp2(a[idx // 512, idx % 128 // 32])


BF16 = ml_dtypes.bfloat16


def bf(x):
    return np.asarray(x, np.float32).astype(BF16)


def f64(x):
    return np.asarray(x).astype(np.float64)


B, N, D_IN, D_H, NM = 4, 512, 256, 256, 5
F = D_IN + D_H


def setup_inputs():
    t = mx_kscale(F)
    return {"x": bf(np.random.standard_normal((B, N, D_IN)) * t[:D_IN]),
            "rh": bf(np.random.standard_normal((B, N, D_H)) * 0.7 * t[D_IN:]),
            "d1_s0": bf(np.random.standard_normal((B, N, F)) * 0.6 * t),
            "d1_s1": bf(np.random.standard_normal((B, N, F)) * 0.6 * t),
            "support0": bf(np.random.standard_normal((N, N)) * 0.7 / np.sqrt(N)),
            "support1": bf(np.random.standard_normal((N, N)) * 0.7 / np.sqrt(N)),
            "cand_w": bf(np.random.standard_normal((NM * F, D_H)) / np.sqrt(NM * F) / np.tile(t, NM)[:, None]),
            "cand_b": bf(0.5 * np.random.standard_normal(D_H)),
            "u": bf(1.0 / (1.0 + np.exp(-(1.0 + np.random.standard_normal((B, N, D_H)))))),
            "h": bf(np.random.standard_normal((B, N, D_H)))}


def reference(x, rh, d1_s0, d1_s1, support0, support1, cand_w, cand_b, u, h):
    x0 = np.concatenate([f64(x), f64(rh)], axis=-1)
    stack = [x0]
    for sup, d1 in ((support0, d1_s0), (support1, d1_s1)):
        x1 = f64(d1)
        x2 = 2.0 * (mxq(f64(sup), 1, "e4m3") @ mxq(x1, 1, "e4m3")) - x0
        stack += [x1, x2]
    x_cat = np.concatenate(stack, axis=-1)
    c = np.tanh((mxq(x_cat, 2, "e4m3") @ mxq(f64(cand_w), 0, "e4m3")) + f64(cand_b))
    u = f64(u)
    return u * f64(h) + (1.0 - u) * c

@@ -1,0 +1,434 @@
+from contextlib import ExitStack
+
+import concourse.mybir as mybir
+from concourse.masks import make_identity
+
+FLOPS = 2 * 2 * 4 * 512 * 512 * 512 + 2 * 2048 * 2560 * 256
+
+BF16 = mybir.dt.bfloat16
+F32 = mybir.dt.float32
+U32 = mybir.dt.uint32
+U8 = mybir.dt.uint8
+FP8X4 = mybir.dt.float8_e4m3fn_x4
+ALU = mybir.AluOpType
+ACT = mybir.ActivationFunctionType
+
+P = 128
+B = 4
+NODES = 512
+F = 512
+DH = 256
+NM = 5
+UNITS = 2 * B
+
+MANUAL = True
+ELAG = 3
+E4_ON_V_FROM = 7
+
+
+def unit(j):
+    return (j // 2, j % 2)
+
+
+def build_queues():
+    pe, sc, ve, gp = [], [], [], []
+
+    def tp(*key):
+        return [("Tp",) + key + (hb,) for hb in range(2)]
+
+    def tcp(*key):
+        return [("Tc",) + key + (hb,) for hb in range(2)]
+
+    pe.extend(tp("sup", 0) + tp("x", 0) + tp("sup", 1) + [("BM",)] + tp("d", 0, 0) + tp("d", 0, 1))
+    sc.extend(tcp("sup", 0) + tcp("x", 0) + tcp("sup", 1) + tcp("d", 0, 0) + tcp("d", 0, 1))
+    ve.extend([("R1", 0, 0), ("Qs", 0), ("QG", 0, 0), ("R1", 0, 1), ("Qs", 1), ("QG", 0, 1), ("QX", 0), ("BC",), ("QD", 0, 0), ("QD", 0, 1)])
+    for k in range(2):
+        for sl in range(2):
+            pe.append(("S1", 0, k, sl))
+    s_chunks = []
+    p_chunks = []
+    for pb in range(1, B):
+        s_chunks.append([("R1", pb, 0), ("R1", pb, 1)])
+        p_chunks.append([])
+        s_chunks.append(tcp("x", pb) + tcp("d", pb, 0) + tcp("d", pb, 1))
+        p_chunks.append(tp("x", pb) + tp("d", pb, 0) + tp("d", pb, 1))
+    gp.append(("E0",) + unit(0))
+    for j in range(-1, UNITS + ELAG + 1):
+        m = j + 1
+        ch = list(s_chunks[m]) if m < len(s_chunks) else []
+        pch = list(p_chunks[m]) if m < len(p_chunks) else []
+        sc.extend(ch[:1])
+        if 0 <= j - 1 < UNITS:
+            sc.append(("TH",) + unit(j - 1))
+        sc.extend(ch[1:])
+        pe.extend(pch)
+        if 0 <= j - ELAG + 1 < UNITS:
+            pe.append(("CB",) + unit(j - ELAG + 1))
+        if 0 <= j and j + 1 < UNITS:
+            bn, hn = unit(j + 1)
+            for k in range(2):
+                for sl in range(2):
+                    pe.append(("S1", bn, k, 2 * hn + sl))
+        if 0 <= j < UNITS:
+            pe.append(("S2",) + unit(j))
+        if 0 <= j - ELAG < UNITS:
+            ve.append(("E3",) + unit(j - ELAG))
+            if j - ELAG >= E4_ON_V_FROM:
+                ve.append(("E4",) + unit(j - ELAG))
+            else:
+                gp.append(("E4",) + unit(j - ELAG))
+            if j - ELAG + 1 < UNITS:
+                gp.append(("E0",) + unit(j - ELAG + 1))
+        if 0 <= j < UNITS:
+            b, hb = unit(j)
+            for k in range(2):
+                for sl in range(2):
+                    ve.append(("X2", b, k, 2 * hb + sl))
+            if j == 0:
+                ve.extend([("R2", g) for g in range(NM)] + [("QW",)])
+            pb = b + 1
+            pq = []
+            if pb < B:
+                pq = [("QG", pb, 0), ("QG", pb, 1)] if hb == 0 else [("QX", pb), ("QD", pb, 0), ("QD", pb, 1)]
+            ve.extend(pq[0:1])
+            ve.append(("QY", b, 0, hb))
+            ve.extend(pq[1:2])
+            ve.append(("QY", b, 1, hb))
+            ve.extend(pq[2:])
+    return [("PE", pe), ("S", sc), ("V", ve), ("G", gp)]
+
+
+def needs_of(op):
+    kind = op[0]
+    a = op[1:]
+    if kind == "Tc":
+        first = [("Tc",) + a[:-1] + (0,)] if a[-1] == 1 else []
+        return [("Tp",) + a] + first
+    if kind == "Qs":
+        return [("Tc", "sup", a[0], hb) for hb in range(2)]
+    if kind == "QG":
+        return [("R1",) + a]
+    if kind == "QX":
+        return [("Tc", "x", a[0], hb) for hb in range(2)]
+    if kind == "QD":
+        return [("Tc", "d", a[0], a[1], hb) for hb in range(2)] + [("QX", a[0])]
+    if kind == "S1":
+        return [("QG", a[0], a[1]), ("Qs", a[1])]
+    if kind == "X2":
+        first = [("X2", a[0], a[1], 2 * (a[2] // 2))] if a[2] % 2 == 1 else []
+        return [("S1",) + a, ("Tc", "x", a[0], a[2] // 2)] + first
+    if kind == "QY":
+        return [("X2", a[0], a[1], 2 * a[2] + sl) for sl in range(2)] + [("QX", a[0])]
+    if kind == "QW":
+        return [("R2", g) for g in range(NM)]
+    if kind == "S2":
+        return [("QW",), ("QX", a[0]), ("QD", a[0], 0), ("QD", a[0], 1), ("QY", a[0], 0, a[1]), ("QY", a[0], 1, a[1])]
+    if kind == "TH":
+        return [("S2",) + a, ("BC",)]
+    if kind == "CB":
+        return [("TH",) + a]
+    if kind == "E3":
+        return [("CB",) + a]
+    if kind == "E4":
+        return [("E3",) + a, ("E0",) + a]
+    if kind == "BC":
+        return [("BM",)]
+    return []
+
+
+def ring_of(op):
+    kind = op[0]
+    a = op[1:]
+    if kind == "Tp":
+        return [("tp", 2, [("Tc",) + a])]
+    if kind == "BM":
+        return [("cb", 1, [("BC",)])]
+    if kind == "Tc" and a[-1] == 0:
+        if a[0] == "sup":
+            return [("grp", 3, [("Qs", a[1])])]
+        if a[0] == "d":
+            return [("grp", 3, [("QD", a[1], a[2])])]
+        return [("x0g", 2, [("QX", a[1])] + [("X2", a[1], k, s) for k in range(2) for s in range(4)])]
+    if kind == "R1":
+        return [("g1", 3, [("QG",) + a])]
+    if kind == "QG":
+        return [("dc", 4, [("S1", a[0], a[1], s) for s in range(4)])]
+    if kind == "S1":
+        return [("y", 4, [("X2",) + a])]
+    if kind == "X2" and a[2] % 2 == 0:
+        return [("x2g", 4, [("QY", a[0], a[1], a[2] // 2)])]
+    if kind == "QX":
+        return [("xc", 2, [("S2", a[0], hb) for hb in range(2)])]
+    if kind == "S2":
+        return [("z", 1, [("TH",) + a])]
+    if kind == "TH":
+        return [("ct", 3, [("CB",) + a])]
+    if kind == "CB":
+        return [("cb", 1, [("E3",) + a])]
+    if kind == "E0":
+        return [("uh", 2, [("E4",) + a])]
+    if kind == "E3":
+        return [("tt", 2, [("E4",) + a])]
+    return []
+
+
+def weave(queues, emit):
+    done = set()
+    heads = [0] * len(queues)
+    taken = {}
+    total = sum(len(q) for (eng, q) in queues)
+    for sweep in range(total):
+        for qi, (eng, q) in enumerate(queues):
+            while heads[qi] < len(q):
+                op = q[heads[qi]]
+                ok = all(n in done for n in needs_of(op))
+                for tag, slots, readers in ring_of(op):
+                    hist = taken.get(tag, [])
+                    if len(hist) >= slots and not all(r in done for r in hist[len(hist) - slots]):
+                        ok = False
+                if not ok:
+                    break
+                for tag, slots, readers in ring_of(op):
+                    taken[tag] = taken.get(tag, []) + [readers]
+                emit(op, eng)
+                done.add(op)
+                heads[qi] += 1
+    assert len(done) == total, "the queues cannot be woven"
+
+
+def tile_dcgrucell_pc_kernel(tc, x, rh, d1_s0, d1_s1, support0, support1, cand_w, cand_b, u, h, out):
+    nc = tc.nc
+    with ExitStack() as ctx:
+        const = ctx.enter_context(tc.tile_pool(name="const", bufs=1))
+        keep = ctx.enter_context(tc.tile_pool(name="keep", bufs=1))
+        work = ctx.enter_context(tc.tile_pool(name="work", bufs=2))
+        psum = ctx.enter_context(tc.psum_pool(name="psum", bufs=1))
+        if MANUAL:
+            ctx.enter_context(tc.manual_schedule())
+
+        def node_view(src):
+            return src.rearrange("(a i e) c -> i a e c", a=2, e=2)
+
+        def slot_view(t):
+            return t.rearrange("p (a e) c -> p a e c", a=2)
+
+        ident = const.tile([P, P], F32, name="ident")
+        make_identity(nc, ident[:])
+        ident_bf = const.tile([P, P], BF16, name="ident_bf")
+        nc.vector.tensor_copy(out=ident_bf[:], in_=ident[:])
+        brow = const.tile([P, P], BF16, name="brow")
+        nc.vector.memset(brow[:], 0.0)
+        bias = const.tile([P, 2], F32, name="bias")
+
+        t = {}
+
+        def load_nodes(key, src, width):
+            t[key] = keep.tile([P, 4, width], BF16, name="in%d" % len(t))
+            nc.sync.dma_start(out=slot_view(t[key][:]), in_=node_view(src))
+
+        d1 = (d1_s0, d1_s1)
+
+        def load_batch(b):
+            load_nodes(("d", b, 0), d1[0][b], F)
+            load_nodes(("d", b, 1), d1[1][b], F)
+            load_nodes(("x", b), x[b], DH)
+            load_nodes(("rh", b), rh[b], DH)
+
+        def load_gate(b):
+            load_nodes(("u", b), u[b], DH)
+            load_nodes(("h", b), h[b], DH)
+
+        load_nodes(("sup", 0), support0, NODES)
+        load_nodes(("d", 0, 0), d1[0][0], F)
+        load_nodes(("x", 0), x[0], DH)
+        load_nodes(("rh", 0), rh[0], DH)
+        nc.sync.dma_start(out=brow[0:2, :], in_=cand_b.rearrange("(t q) -> t q", t=2))
+        load_nodes(("sup", 1), support1, NODES)
+        load_nodes(("d", 0, 1), d1[1][0], F)
+        load_batch(1)
+        w_sb = keep.tile([P, NM, 4, DH], BF16, name="w_sb")
+        nc.sync.dma_start(
+            out=w_sb[:].rearrange("p g (a e) j -> p (g a) (e j)", a=2),
+            in_=cand_w.rearrange("(g a q e) j -> q (g a) (e j)", g=NM, a=2, e=2),
+        )
+        load_gate(0)
+        load_batch(2)
+        load_gate(1)
+        load_batch(3)
+        load_gate(2)
+        load_gate(3)
+
+        wg = keep.tile([P, NM, DH, 4], BF16, align_bytes=64, name="wg")
+        w_c = keep.tile([P, NM, DH], U32, align_bytes=64, name="w_c")
+        w_s = keep.tile([P, NM, DH], U8, align_bytes=64, name="w_s")
+
+        def copy_on(eng, dst, src):
+            if eng == "V":
+                nc.vector.tensor_copy(out=dst, in_=src)
+            else:
+                nc.scalar.copy(out=dst, in_=src)
+
+        def quantise(src, codes, scales):
+            nc.vector.quantize_mx(out=codes.bitcast(FP8X4), scales=scales, in_=src)
+
+        def words_of(key, s, a):
+            if key[0] == "x":
+                src = t[("x", key[1])] if a == 0 else t[("rh", key[1])]
+                return src[:].bitcast(F32)[:, s, :]
+            return t[key][:].bitcast(F32)[:, s, 128 * a : 128 * a + 128]
+
+        def emit(op, eng):
+            kind = op[0]
+            a = op[1:]
+            if kind == "Tp":
+                key, hb = a[:-1], a[-1]
+                bank = psum.tile([P, 2, 256], F32, tag="tp", bufs=2, name="tp")
+                t[("tp",) + a] = bank
+                for sl in range(2):
+                    for w in range(2):
+                        nc.tensor.transpose(bank[:, w, 128 * sl : 128 * sl + 128], words_of(key, 2 * hb + sl, w), ident[:])
+            elif kind == "Tc":
+                key, hb = a[:-1], a[-1]
+                if hb == 0:
+                    if key[0] == "x":
+                        t[("g",) + key] = work.tile([P, NODES, 4], BF16, align_bytes=64, tag="x0g", bufs=2, name="x0g")
+                    else:
+                        t[("g",) + key] = work.tile([P, NODES, 4], BF16, align_bytes=64, tag="grp", bufs=3, name="grp")
+                copy_on(
+                    eng,
+                    t[("g",) + key][:].bitcast(F32)[:, 256 * hb : 256 * hb + 256, :],
+                    t[("tp",) + a][:].rearrange("p w n -> p n w"),
+                )
+            elif kind == "Qs":
+                t[("supc", a[0])] = keep.tile([P, NODES], U32, align_bytes=64, name="supc%d" % a[0])
+                t[("sups", a[0])] = keep.tile([P, NODES], U8, align_bytes=64, name="sups%d" % a[0])
+                quantise(t[("g", "sup", a[0])][:].rearrange("p c v -> p (c v)"), t[("supc", a[0])][:], t[("sups", a[0])][:])
+            elif kind == "R1":
+                b, k = a
+                g1 = work.tile([P, F, 4], BF16, align_bytes=64, tag="g1", bufs=3, name="g1")
+                t[("g1", b, k)] = g1
+                for w in range(2):
+                    copy_on(
+                        eng,
+                        g1[:, 256 * w : 256 * w + 256, :].rearrange("p (e q) s -> p e q s", e=2),
+                        t[("d", b, k)][:, :, 256 * w : 256 * w + 256].rearrange("p s (q e) -> p e q s", e=2),
+                    )
+            elif kind == "QG":
+                t[("dc",) + a] = work.tile([P, F], U32, align_bytes=64, tag="dc", bufs=4, name="dc")
+                t[("ds",) + a] = work.tile([P, F], U8, align_bytes=64, tag="ds", bufs=4, name="ds")
+                quantise(t[("g1",) + a][:].rearrange("p c v -> p (c v)"), t[("dc",) + a][:], t[("ds",) + a][:])
+            elif kind == "QX":
+                b = a[0]
+                t[("xcc", b)] = work.tile([P, NM, NODES], U32, align_bytes=64, tag="xcc", bufs=2, name="xcc")
+                t[("xcs", b)] = work.tile([P, NM, NODES], U8, align_bytes=64, tag="xcs", bufs=2, name="xcs")
+                quantise(t[("g", "x", b)][:].rearrange("p c v -> p (c v)"), t[("xcc", b)][:, 0, :], t[("xcs", b)][:, 0, :])
+            elif kind == "QD":
+                b, k = a
+                quantise(t[("g", "d", b, k)][:].rearrange("p c v -> p (c v)"), t[("xcc", b)][:, 1 + 2 * k, :], t[("xcs", b)][:, 1 + 2 * k, :])
+            elif kind == "S1":
+                b, k, s = a
+                y = psum.tile([P, 4, P], F32, tag="y", bufs=4, name="y")
+                t[("y",) + a] = y
+                cols = slice(128 * s, 128 * s + 128)
+                for v in range(4):
+                    fc = slice(128 * v, 128 * v + 128)
+                    nc.tensor.matmul_mx(
+                        out=y[:, v, :],
+                        lhsT=t[("dc", b, k)][:, fc].bitcast(FP8X4),
+                        lhsT_scale=t[("ds", b, k)][:, fc],
+                        rhs=t[("supc", k)][:, cols].bitcast(FP8X4),
+                        rhs_scale=t[("sups", k)][:, cols],
+                        start=True,
+                        stop=True,
+                    )
+            elif kind == "X2":
+                b, k, s = a
+                hb, sl = s // 2, s % 2
+                if sl == 0:
+                    t[("x2g", b, k, hb)] = work.tile([P, 256, 4], BF16, align_bytes=64, tag="x2g", bufs=4, name="x2g")
+                nc.vector.scalar_tensor_tensor(
+                    out=t[("x2g", b, k, hb)][:, 128 * sl : 128 * sl + 128, :],
+                    in0=t[("y",) + a][:].rearrange("p v n -> p n v"),
+                    scalar=2.0,
+                    in1=t[("g", "x", b)][:, 128 * s : 128 * s + 128, :],
+                    op0=ALU.mult,
+                    op1=ALU.subtract,
+                )
+            elif kind == "QY":
+                b, k, hb = a
+                cols = slice(256 * hb, 256 * hb + 256)
+                quantise(t[("x2g", b, k, hb)][:].rearrange("p c v -> p (c v)"), t[("xcc", b)][:, 2 + 2 * k, cols], t[("xcs", b)][:, 2 + 2 * k, cols])
+            elif kind == "R2":
+                g = a[0]
+                nc.vector.tensor_copy(
+                    out=wg[:, g].rearrange("p (c i) v -> p c v i", i=4),
+                    in_=w_sb[:, g].rearrange("p v (c i) -> p c v i", i=4),
+                )
+            elif kind == "QW":
+                quantise(
+                    wg[:, 0:4].rearrange("p g j v -> p (g j v)"),
+                    w_c[:, 0:4, :].rearrange("p g j -> p (g j)"),
+                    w_s[:, 0:4, :].rearrange("p g j -> p (g j)"),
+                )
+                quantise(wg[:, 4].rearrange("p j v -> p (j v)"), w_c[:, 4, :], w_s[:, 4, :])
+            elif kind == "BM":
+                bp = psum.tile([P, 2, DH], F32, tag="cb", bufs=1, name="bp")
+                t[("bp",)] = bp
+                nc.tensor.matmul(bp[:, 0, 0:P], lhsT=brow[:], rhs=ident_bf[:], start=True, stop=True)
+            elif kind == "BC":
+                nc.vector.tensor_copy(out=bias[:], in_=t[("bp",)][:, 0, 0:2])
+            elif kind == "S2":
+                b, hb = a
+                z = psum.tile([P, 2, DH], F32, tag="z", bufs=1, name="z")
+                t[("z",) + a] = z
+                cols = slice(256 * hb, 256 * hb + 256)
+                for jt in range(2):
+                    jc = slice(128 * jt, 128 * jt + 128)
+                    for g in range(NM):
+                        nc.tensor.matmul_mx(
+                            out=z[:, jt, :],
+                            lhsT=w_c[:, g, jc].bitcast(FP8X4),
+                            lhsT_scale=w_s[:, g, jc],
+                            rhs=t[("xcc", b)][:, g, cols].bitcast(FP8X4),
+                            rhs_scale=t[("xcs", b)][:, g, cols],
+                            start=(g == 0),
+                            stop=(g == NM - 1),
+                        )
+            elif kind == "TH":
+                ct = work.tile([P, 2, DH], F32, tag="ct", bufs=3, name="ct")
+                t[("ct",) + a] = ct
+                for jt in range(2):
+                    nc.scalar.activation(out=ct[:, jt, :], in_=t[("z",) + a][:, jt, :], func=ACT.Tanh, bias=bias[:, jt : jt + 1], scale=1.0)
+            elif kind == "CB":
+                cb = psum.tile([P, 2, DH], F32, tag="cb", bufs=1, name="cb")
+                t[("cb",) + a] = cb
+                for sl in range(2):
+                    for jt in range(2):
+                        nc.tensor.transpose(cb[:, sl, 128 * jt : 128 * jt + 128], t[("ct",) + a][:, jt, 128 * sl : 128 * sl + 128], ident[:])
+            elif kind == "E0":
+                b, hb = a
+                uh = work.tile([P, 2, DH], F32, tag="uh", bufs=2, name="uh")
+                t[("uh",) + a] = uh
+                nc.gpsimd.tensor_tensor(out=uh[:], in0=t[("u", b)][:, 2 * hb : 2 * hb + 2, :], in1=t[("h", b)][:, 2 * hb : 2 * hb + 2, :], op=ALU.mult)
+            elif kind == "E3":
+                b, hb = a
+                tt = work.tile([P, 2, DH], F32, tag="tt", bufs=2, name="tt")
+                t[("tt",) + a] = tt
+                nc.vector.scalar_tensor_tensor(
+                    out=tt[:],
+                    in0=t[("u", b)][:, 2 * hb : 2 * hb + 2, :],
+                    scalar=1.0,
+                    in1=t[("cb",) + a][:],
+                    op0=ALU.subtract,
+                    op1=ALU.mult,
+                )
+            elif kind == "E4":
+                b, hb = a
+                o = work.tile([P, 2, DH], F32, tag="o", bufs=3, name="o")
+                engine = nc.vector if eng == "V" else nc.gpsimd
+                engine.tensor_tensor(out=o[:], in0=t[("uh",) + a][:], in1=t[("tt",) + a][:], op=ALU.subtract)
+                nc.sync.dma_start(out=node_view(out[b])[:, hb, :, :], in_=o[:])
+            else:
+                assert False, "unknown op"
+
+        weave(build_queues(), emit)

@@ -21,7 +21,7 @@ DH = 256
 NM = 5
 UNITS = 2 * B
 
-MANUAL = True
+MANUAL = False
 ELAG = 3
 E4_ON_V_FROM = 7
 

@@ -52,7 +52,6 @@ def build_queues():
         p_chunks.append([])
         s_chunks.append(tcp("x", pb) + tcp("d", pb, 0) + tcp("d", pb, 1))
         p_chunks.append(tp("x", pb) + tp("d", pb, 0) + tp("d", pb, 1))
-    gp.append(("E0",) + unit(0))
     for j in range(-1, UNITS + ELAG + 1):
         m = j + 1
         ch = list(s_chunks[m]) if m < len(s_chunks) else []
@@ -77,8 +76,6 @@ def build_queues():
                 ve.append(("E4",) + unit(j - ELAG))
             else:
                 gp.append(("E4",) + unit(j - ELAG))
-            if j - ELAG + 1 < UNITS:
-                gp.append(("E0",) + unit(j - ELAG + 1))
         if 0 <= j < UNITS:
             b, hb = unit(j)
             for k in range(2):
@@ -130,7 +127,7 @@ def needs_of(op):
     if kind == "E3":
         return [("CB",) + a]
     if kind == "E4":
-        return [("E3",) + a, ("E0",) + a]
+        return [("E3",) + a]
     if kind == "BC":
         return [("BM",)]
     return []
@@ -165,8 +162,6 @@ def ring_of(op):
         return [("ct", 3, [("CB",) + a])]
     if kind == "CB":
         return [("cb", 1, [("E3",) + a])]
-    if kind == "E0":
-        return [("uh", 2, [("E4",) + a])]
     if kind == "E3":
         return [("tt", 2, [("E4",) + a])]
     return []
@@ -376,7 +371,7 @@ def tile_dcgrucell_pc_kernel(tc, x, rh, d1_s0, d1_s1, support0, support1, cand_w
                 t[("bp",)] = bp
                 nc.tensor.matmul(bp[:, 0, 0:P], lhsT=brow[:], rhs=ident_bf[:], start=True, stop=True)
             elif kind == "BC":
-                nc.vector.tensor_copy(out=bias[:], in_=t[("bp",)][:, 0, 0:2])
+                nc.vector.tensor_scalar(out=bias[:], in0=t[("bp",)][:, 0, 0:2], scalar1=-1.0, scalar2=None, op0=ALU.mult)
             elif kind == "S2":
                 b, hb = a
                 z = psum.tile([P, 2, DH], F32, tag="z", bufs=1, name="z")
@@ -398,18 +393,22 @@ def tile_dcgrucell_pc_kernel(tc, x, rh, d1_s0, d1_s1, support0, support1, cand_w
                 ct = work.tile([P, 2, DH], F32, tag="ct", bufs=3, name="ct")
                 t[("ct",) + a] = ct
                 for jt in range(2):
-                    nc.scalar.activation(out=ct[:, jt, :], in_=t[("z",) + a][:, jt, :], func=ACT.Tanh, bias=bias[:, jt : jt + 1], scale=1.0)
+                    nc.scalar.activation(out=ct[:, jt, :], in_=t[("z",) + a][:, jt, :], func=ACT.Tanh, bias=bias[:, jt : jt + 1], scale=-1.0)
             elif kind == "CB":
                 cb = psum.tile([P, 2, DH], F32, tag="cb", bufs=1, name="cb")
                 t[("cb",) + a] = cb
-                for sl in range(2):
-                    for jt in range(2):
-                        nc.tensor.transpose(cb[:, sl, 128 * jt : 128 * jt + 128], t[("ct",) + a][:, jt, 128 * sl : 128 * sl + 128], ident[:])
-            elif kind == "E0":
                 b, hb = a
-                uh = work.tile([P, 2, DH], F32, tag="uh", bufs=2, name="uh")
-                t[("uh",) + a] = uh
-                nc.gpsimd.tensor_tensor(out=uh[:], in0=t[("u", b)][:, 2 * hb : 2 * hb + 2, :], in1=t[("h", b)][:, 2 * hb : 2 * hb + 2, :], op=ALU.mult)
+                for sl in range(2):
+                    nc.tensor.matmul(cb[:, sl, :], lhsT=ident_bf[:], rhs=t[("h", b)][:, 2 * hb + sl, :], start=True, stop=False)
+                    for jt in range(2):
+                        nc.tensor.matmul(
+                            cb[:, sl, 128 * jt : 128 * jt + 128],
+                            lhsT=t[("ct",) + a][:, jt, 128 * sl : 128 * sl + 128],
+                            rhs=ident[:],
+                            start=False,
+                            stop=(jt == 1),
+                            is_transpose=True,
+                        )
             elif kind == "E3":
                 b, hb = a
                 tt = work.tile([P, 2, DH], F32, tag="tt", bufs=2, name="tt")
@@ -426,7 +425,7 @@ def tile_dcgrucell_pc_kernel(tc, x, rh, d1_s0, d1_s1, support0, support1, cand_w
                 b, hb = a
                 o = work.tile([P, 2, DH], F32, tag="o", bufs=3, name="o")
                 engine = nc.vector if eng == "V" else nc.gpsimd
-                engine.tensor_tensor(out=o[:], in0=t[("uh",) + a][:], in1=t[("tt",) + a][:], op=ALU.subtract)
+                engine.tensor_tensor(out=o[:], in0=t[("h", b)][:, 2 * hb : 2 * hb + 2, :], in1=t[("tt",) + a][:], op=ALU.add)
                 nc.sync.dma_start(out=node_view(out[b])[:, hb, :, :], in_=o[:])
             else:
                 assert False, "unknown op"

@@ -305,8 +305,8 @@ def tile_dcgrucell_pc_kernel(tc, x, rh, d1_s0, d1_s1, support0, support1, cand_w
                 for w in range(2):
                     copy_on(
                         eng,
-                        g1[:, 256 * w : 256 * w + 256, :].rearrange("p (e q) s -> p e q s", e=2),
-                        t[("d", b, k)][:, :, 256 * w : 256 * w + 256].rearrange("p s (q e) -> p e q s", e=2),
+                        g1[:, 256 * w : 256 * w + 256, :].rearrange("p (e q) s -> p q s e", e=2),
+                        t[("d", b, k)][:, :, 256 * w : 256 * w + 256].rearrange("p s (q e) -> p q s e", e=2),
                     )
             elif kind == "QG":
                 t[("dc",) + a] = work.tile([P, F], U32, align_bytes=64, tag="dc", bufs=4, name="dc")

from contextlib import ExitStack

import concourse.mybir as mybir
from concourse.masks import make_identity

FLOPS = 2 * 2 * 4 * 512 * 512 * 512 + 2 * 2048 * 2560 * 256

BF16 = mybir.dt.bfloat16
F32 = mybir.dt.float32
U32 = mybir.dt.uint32
U8 = mybir.dt.uint8
FP8X4 = mybir.dt.float8_e4m3fn_x4
ALU = mybir.AluOpType
ACT = mybir.ActivationFunctionType

P = 128
B = 4
NODES = 512
F = 512
DH = 256
NM = 5
UNITS = 2 * B

MANUAL = False
ELAG = 3
E4_ON_V_FROM = 7


def unit(j):
    return (j // 2, j % 2)


def build_queues():
    pe, sc, ve, gp = [], [], [], []

    def tp(*key):
        return [("Tp",) + key + (hb,) for hb in range(2)]

    def tcp(*key):
        return [("Tc",) + key + (hb,) for hb in range(2)]

    pe.extend(tp("sup", 0) + tp("x", 0) + tp("sup", 1) + [("BM",)] + tp("d", 0, 0) + tp("d", 0, 1))
    sc.extend(tcp("sup", 0) + tcp("x", 0) + tcp("sup", 1) + tcp("d", 0, 0) + tcp("d", 0, 1))
    ve.extend([("R1", 0, 0), ("Qs", 0), ("QG", 0, 0), ("R1", 0, 1), ("Qs", 1), ("QG", 0, 1), ("QX", 0), ("BC",), ("QD", 0, 0), ("QD", 0, 1)])
    for k in range(2):
        for sl in range(2):
            pe.append(("S1", 0, k, sl))
    s_chunks = []
    p_chunks = []
    for pb in range(1, B):
        s_chunks.append([("R1", pb, 0), ("R1", pb, 1)])
        p_chunks.append([])
        s_chunks.append(tcp("x", pb) + tcp("d", pb, 0) + tcp("d", pb, 1))
        p_chunks.append(tp("x", pb) + tp("d", pb, 0) + tp("d", pb, 1))
    for j in range(-1, UNITS + ELAG + 1):
        m = j + 1
        ch = list(s_chunks[m]) if m < len(s_chunks) else []
        pch = list(p_chunks[m]) if m < len(p_chunks) else []
        sc.extend(ch[:1])
        if 0 <= j - 1 < UNITS:
            sc.append(("TH",) + unit(j - 1))
        sc.extend(ch[1:])
        pe.extend(pch)
        if 0 <= j - ELAG + 1 < UNITS:
            pe.append(("CB",) + unit(j - ELAG + 1))
        if 0 <= j and j + 1 < UNITS:
            bn, hn = unit(j + 1)
            for k in range(2):
                for sl in range(2):
                    pe.append(("S1", bn, k, 2 * hn + sl))
        if 0 <= j < UNITS:
            pe.append(("S2",) + unit(j))
        if 0 <= j - ELAG < UNITS:
            ve.append(("E3",) + unit(j - ELAG))
            if j - ELAG >= E4_ON_V_FROM:
                ve.append(("E4",) + unit(j - ELAG))
            else:
                gp.append(("E4",) + unit(j - ELAG))
        if 0 <= j < UNITS:
            b, hb = unit(j)
            for k in range(2):
                for sl in range(2):
                    ve.append(("X2", b, k, 2 * hb + sl))
            if j == 0:
                ve.extend([("R2", g) for g in range(NM)] + [("QW",)])
            pb = b + 1
            pq = []
            if pb < B:
                pq = [("QG", pb, 0), ("QG", pb, 1)] if hb == 0 else [("QX", pb), ("QD", pb, 0), ("QD", pb, 1)]
            ve.extend(pq[0:1])
            ve.append(("QY", b, 0, hb))
            ve.extend(pq[1:2])
            ve.append(("QY", b, 1, hb))
            ve.extend(pq[2:])
    return [("PE", pe), ("S", sc), ("V", ve), ("G", gp)]


def needs_of(op):
    kind = op[0]
    a = op[1:]
    if kind == "Tc":
        first = [("Tc",) + a[:-1] + (0,)] if a[-1] == 1 else []
        return [("Tp",) + a] + first
    if kind == "Qs":
        return [("Tc", "sup", a[0], hb) for hb in range(2)]
    if kind == "QG":
        return [("R1",) + a]
    if kind == "QX":
        return [("Tc", "x", a[0], hb) for hb in range(2)]
    if kind == "QD":
        return [("Tc", "d", a[0], a[1], hb) for hb in range(2)] + [("QX", a[0])]
    if kind == "S1":
        return [("QG", a[0], a[1]), ("Qs", a[1])]
    if kind == "X2":
        first = [("X2", a[0], a[1], 2 * (a[2] // 2))] if a[2] % 2 == 1 else []
        return [("S1",) + a, ("Tc", "x", a[0], a[2] // 2)] + first
    if kind == "QY":
        return [("X2", a[0], a[1], 2 * a[2] + sl) for sl in range(2)] + [("QX", a[0])]
    if kind == "QW":
        return [("R2", g) for g in range(NM)]
    if kind == "S2":
        return [("QW",), ("QX", a[0]), ("QD", a[0], 0), ("QD", a[0], 1), ("QY", a[0], 0, a[1]), ("QY", a[0], 1, a[1])]
    if kind == "TH":
        return [("S2",) + a, ("BC",)]
    if kind == "CB":
        return [("TH",) + a]
    if kind == "E3":
        return [("CB",) + a]
    if kind == "E4":
        return [("E3",) + a]
    if kind == "BC":
        return [("BM",)]
    return []


def ring_of(op):
    kind = op[0]
    a = op[1:]
    if kind == "Tp":
        return [("tp", 2, [("Tc",) + a])]
    if kind == "BM":
        return [("cb", 1, [("BC",)])]
    if kind == "Tc" and a[-1] == 0:
        if a[0] == "sup":
            return [("grp", 3, [("Qs", a[1])])]
        if a[0] == "d":
            return [("grp", 3, [("QD", a[1], a[2])])]
        return [("x0g", 2, [("QX", a[1])] + [("X2", a[1], k, s) for k in range(2) for s in range(4)])]
    if kind == "R1":
        return [("g1", 3, [("QG",) + a])]
    if kind == "QG":
        return [("dc", 4, [("S1", a[0], a[1], s) for s in range(4)])]
    if kind == "S1":
        return [("y", 4, [("X2",) + a])]
    if kind == "X2" and a[2] % 2 == 0:
        return [("x2g", 4, [("QY", a[0], a[1], a[2] // 2)])]
    if kind == "QX":
        return [("xc", 2, [("S2", a[0], hb) for hb in range(2)])]
    if kind == "S2":
        return [("z", 1, [("TH",) + a])]
    if kind == "TH":
        return [("ct", 3, [("CB",) + a])]
    if kind == "CB":
        return [("cb", 1, [("E3",) + a])]
    if kind == "E3":
        return [("tt", 2, [("E4",) + a])]
    return []


def weave(queues, emit):
    done = set()
    heads = [0] * len(queues)
    taken = {}
    total = sum(len(q) for (eng, q) in queues)
    for sweep in range(total):
        for qi, (eng, q) in enumerate(queues):
            while heads[qi] < len(q):
                op = q[heads[qi]]
                ok = all(n in done for n in needs_of(op))
                for tag, slots, readers in ring_of(op):
                    hist = taken.get(tag, [])
                    if len(hist) >= slots and not all(r in done for r in hist[len(hist) - slots]):
                        ok = False
                if not ok:
                    break
                for tag, slots, readers in ring_of(op):
                    taken[tag] = taken.get(tag, []) + [readers]
                emit(op, eng)
                done.add(op)
                heads[qi] += 1
    assert len(done) == total, "the queues cannot be woven"


def tile_dcgrucell_pc_kernel(tc, x, rh, d1_s0, d1_s1, support0, support1, cand_w, cand_b, u, h, out):
    nc = tc.nc
    with ExitStack() as ctx:
        const = ctx.enter_context(tc.tile_pool(name="const", bufs=1))
        keep = ctx.enter_context(tc.tile_pool(name="keep", bufs=1))
        work = ctx.enter_context(tc.tile_pool(name="work", bufs=2))
        psum = ctx.enter_context(tc.psum_pool(name="psum", bufs=1))
        if MANUAL:
            ctx.enter_context(tc.manual_schedule())

        def node_view(src):
            return src.rearrange("(a i e) c -> i a e c", a=2, e=2)

        def slot_view(t):
            return t.rearrange("p (a e) c -> p a e c", a=2)

        ident = const.tile([P, P], F32, name="ident")
        make_identity(nc, ident[:])
        ident_bf = const.tile([P, P], BF16, name="ident_bf")
        nc.vector.tensor_copy(out=ident_bf[:], in_=ident[:])
        brow = const.tile([P, P], BF16, name="brow")
        nc.vector.memset(brow[:], 0.0)
        bias = const.tile([P, 2], F32, name="bias")

        t = {}

        def load_nodes(key, src, width):
            t[key] = keep.tile([P, 4, width], BF16, name="in%d" % len(t))
            nc.sync.dma_start(out=slot_view(t[key][:]), in_=node_view(src))

        d1 = (d1_s0, d1_s1)

        def load_batch(b):
            load_nodes(("d", b, 0), d1[0][b], F)
            load_nodes(("d", b, 1), d1[1][b], F)
            load_nodes(("x", b), x[b], DH)
            load_nodes(("rh", b), rh[b], DH)

        def load_gate(b):
            load_nodes(("u", b), u[b], DH)
            load_nodes(("h", b), h[b], DH)

        load_nodes(("sup", 0), support0, NODES)
        load_nodes(("d", 0, 0), d1[0][0], F)
        load_nodes(("x", 0), x[0], DH)
        load_nodes(("rh", 0), rh[0], DH)
        nc.sync.dma_start(out=brow[0:2, :], in_=cand_b.rearrange("(t q) -> t q", t=2))
        load_nodes(("sup", 1), support1, NODES)
        load_nodes(("d", 0, 1), d1[1][0], F)
        load_batch(1)
        w_sb = keep.tile([P, NM, 4, DH], BF16, name="w_sb")
        nc.sync.dma_start(
            out=w_sb[:].rearrange("p g (a e) j -> p (g a) (e j)", a=2),
            in_=cand_w.rearrange("(g a q e) j -> q (g a) (e j)", g=NM, a=2, e=2),
        )
        load_gate(0)
        load_batch(2)
        load_gate(1)
        load_batch(3)
        load_gate(2)
        load_gate(3)

        wg = keep.tile([P, NM, DH, 4], BF16, align_bytes=64, name="wg")
        w_c = keep.tile([P, NM, DH], U32, align_bytes=64, name="w_c")
        w_s = keep.tile([P, NM, DH], U8, align_bytes=64, name="w_s")

        def copy_on(eng, dst, src):
            if eng == "V":
                nc.vector.tensor_copy(out=dst, in_=src)
            else:
                nc.scalar.copy(out=dst, in_=src)

        def quantise(src, codes, scales):
            nc.vector.quantize_mx(out=codes.bitcast(FP8X4), scales=scales, in_=src)

        def words_of(key, s, a):
            if key[0] == "x":
                src = t[("x", key[1])] if a == 0 else t[("rh", key[1])]
                return src[:].bitcast(F32)[:, s, :]
            return t[key][:].bitcast(F32)[:, s, 128 * a : 128 * a + 128]

        def emit(op, eng):
            kind = op[0]
            a = op[1:]
            if kind == "Tp":
                key, hb = a[:-1], a[-1]
                bank = psum.tile([P, 2, 256], F32, tag="tp", bufs=2, name="tp")
                t[("tp",) + a] = bank
                for sl in range(2):
                    for w in range(2):
                        nc.tensor.transpose(bank[:, w, 128 * sl : 128 * sl + 128], words_of(key, 2 * hb + sl, w), ident[:])
            elif kind == "Tc":
                key, hb = a[:-1], a[-1]
                if hb == 0:
                    if key[0] == "x":
                        t[("g",) + key] = work.tile([P, NODES, 4], BF16, align_bytes=64, tag="x0g", bufs=2, name="x0g")
                    else:
                        t[("g",) + key] = work.tile([P, NODES, 4], BF16, align_bytes=64, tag="grp", bufs=3, name="grp")
                copy_on(
                    eng,
                    t[("g",) + key][:].bitcast(F32)[:, 256 * hb : 256 * hb + 256, :],
                    t[("tp",) + a][:].rearrange("p w n -> p n w"),
                )
            elif kind == "Qs":
                t[("supc", a[0])] = keep.tile([P, NODES], U32, align_bytes=64, name="supc%d" % a[0])
                t[("sups", a[0])] = keep.tile([P, NODES], U8, align_bytes=64, name="sups%d" % a[0])
                quantise(t[("g", "sup", a[0])][:].rearrange("p c v -> p (c v)"), t[("supc", a[0])][:], t[("sups", a[0])][:])
            elif kind == "R1":
                b, k = a
                g1 = work.tile([P, F, 4], BF16, align_bytes=64, tag="g1", bufs=3, name="g1")
                t[("g1", b, k)] = g1
                for w in range(2):
                    copy_on(
                        eng,
                        g1[:, 256 * w : 256 * w + 256, :].rearrange("p (e q) s -> p q s e", e=2),
                        t[("d", b, k)][:, :, 256 * w : 256 * w + 256].rearrange("p s (q e) -> p q s e", e=2),
                    )
            elif kind == "QG":
                t[("dc",) + a] = work.tile([P, F], U32, align_bytes=64, tag="dc", bufs=4, name="dc")
                t[("ds",) + a] = work.tile([P, F], U8, align_bytes=64, tag="ds", bufs=4, name="ds")
                quantise(t[("g1",) + a][:].rearrange("p c v -> p (c v)"), t[("dc",) + a][:], t[("ds",) + a][:])
            elif kind == "QX":
                b = a[0]
                t[("xcc", b)] = work.tile([P, NM, NODES], U32, align_bytes=64, tag="xcc", bufs=2, name="xcc")
                t[("xcs", b)] = work.tile([P, NM, NODES], U8, align_bytes=64, tag="xcs", bufs=2, name="xcs")
                quantise(t[("g", "x", b)][:].rearrange("p c v -> p (c v)"), t[("xcc", b)][:, 0, :], t[("xcs", b)][:, 0, :])
            elif kind == "QD":
                b, k = a
                quantise(t[("g", "d", b, k)][:].rearrange("p c v -> p (c v)"), t[("xcc", b)][:, 1 + 2 * k, :], t[("xcs", b)][:, 1 + 2 * k, :])
            elif kind == "S1":
                b, k, s = a
                y = psum.tile([P, 4, P], F32, tag="y", bufs=4, name="y")
                t[("y",) + a] = y
                cols = slice(128 * s, 128 * s + 128)
                for v in range(4):
                    fc = slice(128 * v, 128 * v + 128)
                    nc.tensor.matmul_mx(
                        out=y[:, v, :],
                        lhsT=t[("dc", b, k)][:, fc].bitcast(FP8X4),
                        lhsT_scale=t[("ds", b, k)][:, fc],
                        rhs=t[("supc", k)][:, cols].bitcast(FP8X4),
                        rhs_scale=t[("sups", k)][:, cols],
                        start=True,
                        stop=True,
                    )
            elif kind == "X2":
                b, k, s = a
                hb, sl = s // 2, s % 2
                if sl == 0:
                    t[("x2g", b, k, hb)] = work.tile([P, 256, 4], BF16, align_bytes=64, tag="x2g", bufs=4, name="x2g")
                nc.vector.scalar_tensor_tensor(
                    out=t[("x2g", b, k, hb)][:, 128 * sl : 128 * sl + 128, :],
                    in0=t[("y",) + a][:].rearrange("p v n -> p n v"),
                    scalar=2.0,
                    in1=t[("g", "x", b)][:, 128 * s : 128 * s + 128, :],
                    op0=ALU.mult,
                    op1=ALU.subtract,
                )
            elif kind == "QY":
                b, k, hb = a
                cols = slice(256 * hb, 256 * hb + 256)
                quantise(t[("x2g", b, k, hb)][:].rearrange("p c v -> p (c v)"), t[("xcc", b)][:, 2 + 2 * k, cols], t[("xcs", b)][:, 2 + 2 * k, cols])
            elif kind == "R2":
                g = a[0]
                nc.vector.tensor_copy(
                    out=wg[:, g].rearrange("p (c i) v -> p c v i", i=4),
                    in_=w_sb[:, g].rearrange("p v (c i) -> p c v i", i=4),
                )
            elif kind == "QW":
                quantise(
                    wg[:, 0:4].rearrange("p g j v -> p (g j v)"),
                    w_c[:, 0:4, :].rearrange("p g j -> p (g j)"),
                    w_s[:, 0:4, :].rearrange("p g j -> p (g j)"),
                )
                quantise(wg[:, 4].rearrange("p j v -> p (j v)"), w_c[:, 4, :], w_s[:, 4, :])
            elif kind == "BM":
                bp = psum.tile([P, 2, DH], F32, tag="cb", bufs=1, name="bp")
                t[("bp",)] = bp
                nc.tensor.matmul(bp[:, 0, 0:P], lhsT=brow[:], rhs=ident_bf[:], start=True, stop=True)
            elif kind == "BC":
                nc.vector.tensor_scalar(out=bias[:], in0=t[("bp",)][:, 0, 0:2], scalar1=-1.0, scalar2=None, op0=ALU.mult)
            elif kind == "S2":
                b, hb = a
                z = psum.tile([P, 2, DH], F32, tag="z", bufs=1, name="z")
                t[("z",) + a] = z
                cols = slice(256 * hb, 256 * hb + 256)
                for jt in range(2):
                    jc = slice(128 * jt, 128 * jt + 128)
                    for g in range(NM):
                        nc.tensor.matmul_mx(
                            out=z[:, jt, :],
                            lhsT=w_c[:, g, jc].bitcast(FP8X4),
                            lhsT_scale=w_s[:, g, jc],
                            rhs=t[("xcc", b)][:, g, cols].bitcast(FP8X4),
                            rhs_scale=t[("xcs", b)][:, g, cols],
                            start=(g == 0),
                            stop=(g == NM - 1),
                        )
            elif kind == "TH":
                ct = work.tile([P, 2, DH], F32, tag="ct", bufs=3, name="ct")
                t[("ct",) + a] = ct
                for jt in range(2):
                    nc.scalar.activation(out=ct[:, jt, :], in_=t[("z",) + a][:, jt, :], func=ACT.Tanh, bias=bias[:, jt : jt + 1], scale=-1.0)
            elif kind == "CB":
                cb = psum.tile([P, 2, DH], F32, tag="cb", bufs=1, name="cb")
                t[("cb",) + a] = cb
                b, hb = a
                for sl in range(2):
                    nc.tensor.matmul(cb[:, sl, :], lhsT=ident_bf[:], rhs=t[("h", b)][:, 2 * hb + sl, :], start=True, stop=False)
                    for jt in range(2):
                        nc.tensor.matmul(
                            cb[:, sl, 128 * jt : 128 * jt + 128],
                            lhsT=t[("ct",) + a][:, jt, 128 * sl : 128 * sl + 128],
                            rhs=ident[:],
                            start=False,
                            stop=(jt == 1),
                            is_transpose=True,
                        )
            elif kind == "E3":
                b, hb = a
                tt = work.tile([P, 2, DH], F32, tag="tt", bufs=2, name="tt")
                t[("tt",) + a] = tt
                nc.vector.scalar_tensor_tensor(
                    out=tt[:],
                    in0=t[("u", b)][:, 2 * hb : 2 * hb + 2, :],
                    scalar=1.0,
                    in1=t[("cb",) + a][:],
                    op0=ALU.subtract,
                    op1=ALU.mult,
                )
            elif kind == "E4":
                b, hb = a
                o = work.tile([P, 2, DH], F32, tag="o", bufs=3, name="o")
                engine = nc.vector if eng == "V" else nc.gpsimd
                engine.tensor_tensor(out=o[:], in0=t[("h", b)][:, 2 * hb : 2 * hb + 2, :], in1=t[("tt",) + a][:], op=ALU.add)
                nc.sync.dma_start(out=node_view(out[b])[:, hb, :, :], in_=o[:])
            else:
                assert False, "unknown op"

        weave(build_queues(), emit)
